import numpy as np
import ml_dtypes

BF16 = ml_dtypes.bfloat16


def bf(x):
    return np.asarray(x, np.float32).astype(BF16)


def f32(x):
    return np.asarray(x, np.float32)


def f64(x):
    return np.asarray(x).astype(np.float64)


def striped(idx):
    return np.tile(idx.reshape(-1, 16).T, (8, 1))


C, HALF, D, S, N, GRID = 768, 384, 128, 256, 512, 30
ROPE_BASE = 10000.0


def grid_draw():
    return np.random.permutation(np.tile(np.arange(GRID), N // GRID + 1))[:N]


def setup_inputs():
    table = f32(np.random.standard_normal((C, S)))
    pos = f32(np.stack([grid_draw(), grid_draw(), np.arange(N)]))
    freq = f32(ROPE_BASE ** (-np.arange(D)[:, None] / D))
    return {"table": table, "pos": pos, "freq": freq, "offs": striped(np.random.permutation(np.tile(np.arange(S), 2))[:N])}


def reference(table, pos, freq, offs):
    idx = offs[:16].T.reshape(-1)
    e = f64(table)[:, idx]
    p = f64(pos)
    u = p / p.max(axis=1, keepdims=True)
    ang = (u[:, None, :] * f64(freq)[None, :, :]).reshape(HALF, N)
    ang = np.concatenate([ang, ang], axis=0)
    rot = np.concatenate([-e[HALF:], e[:HALF]], axis=0)
    return e * np.cos(ang) + rot * np.sin(ang)

@@ -1,0 +1,76 @@
+import math
+
+import concourse.mybir as mybir
+
+F32 = mybir.dt.float32
+U16 = mybir.dt.uint16
+MULT = mybir.AluOpType.mult
+ADD = mybir.AluOpType.add
+SUBTRACT = mybir.AluOpType.subtract
+MAX = mybir.AluOpType.max
+SIN = mybir.ActivationFunctionType.Sin
+
+P = 128
+WORDS = 256
+TOKENS = 512
+AXES = 3
+PIECE = 256
+PER_COLUMN = 16
+
+
+def tile_arcembedding_kernel(tc, table, pos, freq, offs, out):
+    nc = tc.nc
+    with (
+        tc.tile_pool(name="held", bufs=1) as held,
+        tc.tile_pool(name="work", bufs=3) as work,
+    ):
+        offsets = held.tile([P, TOKENS // PER_COLUMN], U16, name="offsets")
+        nc.sync.dma_start(offsets[:], offs)
+        pitch = held.tile([P, 1], F32, name="pitch")
+        nc.scalar.dma_start(pitch[:], freq)
+        places = [held.tile([P, TOKENS], F32, name=f"place{a}") for a in range(AXES)]
+        for a in range(AXES):
+            nc.sync.dma_start(places[a][:], pos[a, :].partition_broadcast(P))
+        words = [held.tile([P, WORDS], F32, name=f"words{b}") for b in range(2 * AXES)]
+        for a in range(AXES):
+            for b in (a, a + AXES):
+                nc.sync.dma_start(words[b][:], table[b * P : (b + 1) * P, :])
+
+        quarter_turn = held.tile([P, 1], F32, name="quarter_turn")
+        nc.vector.memset(quarter_turn[:], math.pi / 2)
+
+        cosines, sines = [], []
+        for a in range(AXES):
+            top = held.tile([P, 1], F32, name=f"top{a}")
+            nc.vector.tensor_reduce(top[:], places[a][:], mybir.AxisListType.X, MAX)
+            rate = held.tile([P, 1], F32, name=f"rate{a}")
+            nc.vector.reciprocal(rate[:], top[:])
+            nc.vector.tensor_tensor(rate[:], rate[:], pitch[:], MULT)
+            cosine = held.tile([P, TOKENS], F32, name=f"cosine{a}")
+            nc.scalar.activation(cosine[:], places[a][:], SIN, bias=quarter_turn[:], scale=rate[:])
+            sine = held.tile([P, TOKENS], F32, name=f"sine{a}")
+            nc.scalar.activation(sine[:], places[a][:], SIN, scale=rate[:])
+            cosines.append(cosine)
+            sines.append(sine)
+
+        for a in range(AXES):
+            low, high = words[a], words[a + AXES]
+            for start in range(0, TOKENS, PIECE):
+                cols = slice(start, start + PIECE)
+                picks = offsets[:, start // PER_COLUMN : (start + PIECE) // PER_COLUMN]
+
+                low_cos = work.tile([P, PIECE], F32, name="low_cos")
+                nc.vector.tensor_tensor(low_cos[:], low[:].indirect(picks), cosines[a][:, cols], MULT)
+                high_sin = work.tile([P, PIECE], F32, name="high_sin")
+                nc.vector.tensor_tensor(high_sin[:], high[:].indirect(picks), sines[a][:, cols], MULT)
+                low_out = work.tile([P, PIECE], F32, name="low_out")
+                nc.vector.tensor_tensor(low_out[:], low_cos[:], high_sin[:], SUBTRACT)
+                nc.sync.dma_start(out[a * P : (a + 1) * P, cols], low_out[:])
+
+                high_cos = work.tile([P, PIECE], F32, name="high_cos")
+                nc.vector.tensor_tensor(high_cos[:], high[:].indirect(picks), cosines[a][:, cols], MULT)
+                low_sin = work.tile([P, PIECE], F32, name="low_sin")
+                nc.vector.tensor_tensor(low_sin[:], low[:].indirect(picks), sines[a][:, cols], MULT)
+                high_out = work.tile([P, PIECE], F32, name="high_out")
+                nc.vector.tensor_tensor(high_out[:], high_cos[:], low_sin[:], ADD)
+                nc.sync.dma_start(out[(a + AXES) * P : (a + AXES + 1) * P, cols], high_out[:])

@@ -1,12 +1,11 @@
 import math
 
 import concourse.mybir as mybir
+from concourse.masks import make_identity
 
 F32 = mybir.dt.float32
 U16 = mybir.dt.uint16
 MULT = mybir.AluOpType.mult
-ADD = mybir.AluOpType.add
-SUBTRACT = mybir.AluOpType.subtract
 MAX = mybir.AluOpType.max
 SIN = mybir.ActivationFunctionType.Sin
 
@@ -22,7 +21,8 @@ def tile_arcembedding_kernel(tc, table, pos, freq, offs, out):
     nc = tc.nc
     with (
         tc.tile_pool(name="held", bufs=1) as held,
-        tc.tile_pool(name="work", bufs=3) as work,
+        tc.tile_pool(name="work", bufs=4) as work,
+        tc.psum_pool(name="sums", bufs=4) as sums,
     ):
         offsets = held.tile([P, TOKENS // PER_COLUMN], U16, name="offsets")
         nc.sync.dma_start(offsets[:], offs)
@@ -35,6 +35,20 @@ def tile_arcembedding_kernel(tc, table, pos, freq, offs, out):
         for a in range(AXES):
             for b in (a, a + AXES):
                 nc.sync.dma_start(words[b][:], table[b * P : (b + 1) * P, :])
+
+        plus = held.tile([P, P], F32, name="plus")
+        make_identity(nc, plus[:])
+        minus = held.tile([P, P], F32, name="minus")
+        nc.gpsimd.memset(minus[:], 0.0)
+        nc.gpsimd.affine_select(
+            out=minus[:],
+            in_=minus[:],
+            compare_op=mybir.AluOpType.not_equal,
+            fill=-1.0,
+            base=0,
+            pattern=[[-1, P]],
+            channel_multiplier=1,
+        )
 
         quarter_turn = held.tile([P, 1], F32, name="quarter_turn")
         nc.vector.memset(quarter_turn[:], math.pi / 2)
@@ -63,14 +77,20 @@ def tile_arcembedding_kernel(tc, table, pos, freq, offs, out):
                 nc.vector.tensor_tensor(low_cos[:], low[:].indirect(picks), cosines[a][:, cols], MULT)
                 high_sin = work.tile([P, PIECE], F32, name="high_sin")
                 nc.vector.tensor_tensor(high_sin[:], high[:].indirect(picks), sines[a][:, cols], MULT)
+                low_sum = sums.tile([P, PIECE], F32, name="low_sum")
+                nc.tensor.matmul(low_sum[:], plus[:], low_cos[:], start=True, stop=False)
+                nc.tensor.matmul(low_sum[:], minus[:], high_sin[:], start=False, stop=True)
                 low_out = work.tile([P, PIECE], F32, name="low_out")
-                nc.vector.tensor_tensor(low_out[:], low_cos[:], high_sin[:], SUBTRACT)
+                nc.scalar.copy(low_out[:], low_sum[:])
                 nc.sync.dma_start(out[a * P : (a + 1) * P, cols], low_out[:])
 
                 high_cos = work.tile([P, PIECE], F32, name="high_cos")
                 nc.vector.tensor_tensor(high_cos[:], high[:].indirect(picks), cosines[a][:, cols], MULT)
                 low_sin = work.tile([P, PIECE], F32, name="low_sin")
                 nc.vector.tensor_tensor(low_sin[:], low[:].indirect(picks), sines[a][:, cols], MULT)
+                high_sum = sums.tile([P, PIECE], F32, name="high_sum")
+                nc.tensor.matmul(high_sum[:], plus[:], high_cos[:], start=True, stop=False)
+                nc.tensor.matmul(high_sum[:], plus[:], low_sin[:], start=False, stop=True)
                 high_out = work.tile([P, PIECE], F32, name="high_out")
-                nc.vector.tensor_tensor(high_out[:], high_cos[:], low_sin[:], ADD)
+                nc.scalar.copy(high_out[:], high_sum[:])
                 nc.sync.dma_start(out[(a + AXES) * P : (a + AXES + 1) * P, cols], high_out[:])

@@ -6,6 +6,7 @@ from concourse.masks import make_identity
 F32 = mybir.dt.float32
 U16 = mybir.dt.uint16
 MULT = mybir.AluOpType.mult
+ADD = mybir.AluOpType.add
 MAX = mybir.AluOpType.max
 SIN = mybir.ActivationFunctionType.Sin
 
@@ -17,22 +18,36 @@ PIECE = 256
 PER_COLUMN = 16
 
 
+def cosine_and_sine(nc, pool, place, pitch, quarter_turn, a):
+    top = pool.tile([P, 1], F32, name=f"top{a}")
+    nc.vector.tensor_reduce(top[:], place[:], mybir.AxisListType.X, MAX)
+    rate = pool.tile([P, 1], F32, name=f"rate{a}")
+    nc.vector.reciprocal(rate[:], top[:])
+    nc.vector.tensor_tensor(rate[:], rate[:], pitch[:], MULT)
+    cosine = pool.tile([P, TOKENS], F32, name=f"cosine{a}")
+    sine = pool.tile([P, TOKENS], F32, name=f"sine{a}")
+    for start in range(0, TOKENS, PIECE):
+        cols = slice(start, start + PIECE)
+        nc.scalar.activation(cosine[:, cols], place[:, cols], SIN, bias=quarter_turn[:], scale=rate[:])
+        nc.scalar.activation(sine[:, cols], place[:, cols], SIN, scale=rate[:])
+    return cosine, sine
+
+
 def tile_arcembedding_kernel(tc, table, pos, freq, offs, out):
     nc = tc.nc
     with (
         tc.tile_pool(name="held", bufs=1) as held,
-        tc.tile_pool(name="work", bufs=4) as work,
-        tc.psum_pool(name="sums", bufs=4) as sums,
+        tc.tile_pool(name="work", bufs=6) as work,
+        tc.psum_pool(name="sums", bufs=6) as sums,
     ):
         offsets = held.tile([P, TOKENS // PER_COLUMN], U16, name="offsets")
         nc.sync.dma_start(offsets[:], offs)
         pitch = held.tile([P, 1], F32, name="pitch")
         nc.scalar.dma_start(pitch[:], freq)
         places = [held.tile([P, TOKENS], F32, name=f"place{a}") for a in range(AXES)]
-        for a in range(AXES):
-            nc.sync.dma_start(places[a][:], pos[a, :].partition_broadcast(P))
         words = [held.tile([P, WORDS], F32, name=f"words{b}") for b in range(2 * AXES)]
         for a in range(AXES):
+            nc.sync.dma_start(places[a][:], pos[a, :].partition_broadcast(P))
             for b in (a, a + AXES):
                 nc.sync.dma_start(words[b][:], table[b * P : (b + 1) * P, :])
 
@@ -49,48 +64,31 @@ def tile_arcembedding_kernel(tc, table, pos, freq, offs, out):
             pattern=[[-1, P]],
             channel_multiplier=1,
         )
-
         quarter_turn = held.tile([P, 1], F32, name="quarter_turn")
         nc.vector.memset(quarter_turn[:], math.pi / 2)
+        first_sine = held.tile([P, 1], F32, name="first_sine")
+        nc.scalar.activation(first_sine[:], quarter_turn[:], SIN)
 
-        cosines, sines = [], []
+        last_sum = (2 * AXES - 1, TOKENS - PIECE)
+        turns = [cosine_and_sine(nc, held, places[0], pitch, quarter_turn, 0)]
         for a in range(AXES):
-            top = held.tile([P, 1], F32, name=f"top{a}")
-            nc.vector.tensor_reduce(top[:], places[a][:], mybir.AxisListType.X, MAX)
-            rate = held.tile([P, 1], F32, name=f"rate{a}")
-            nc.vector.reciprocal(rate[:], top[:])
-            nc.vector.tensor_tensor(rate[:], rate[:], pitch[:], MULT)
-            cosine = held.tile([P, TOKENS], F32, name=f"cosine{a}")
-            nc.scalar.activation(cosine[:], places[a][:], SIN, bias=quarter_turn[:], scale=rate[:])
-            sine = held.tile([P, TOKENS], F32, name=f"sine{a}")
-            nc.scalar.activation(sine[:], places[a][:], SIN, scale=rate[:])
-            cosines.append(cosine)
-            sines.append(sine)
-
-        for a in range(AXES):
-            low, high = words[a], words[a + AXES]
+            cosine, sine = turns[a]
             for start in range(0, TOKENS, PIECE):
+                if start == PIECE and a + 1 < AXES:
+                    turns.append(cosine_and_sine(nc, held, places[a + 1], pitch, quarter_turn, a + 1))
                 cols = slice(start, start + PIECE)
                 picks = offsets[:, start // PER_COLUMN : (start + PIECE) // PER_COLUMN]
-
-                low_cos = work.tile([P, PIECE], F32, name="low_cos")
-                nc.vector.tensor_tensor(low_cos[:], low[:].indirect(picks), cosines[a][:, cols], MULT)
-                high_sin = work.tile([P, PIECE], F32, name="high_sin")
-                nc.vector.tensor_tensor(high_sin[:], high[:].indirect(picks), sines[a][:, cols], MULT)
-                low_sum = sums.tile([P, PIECE], F32, name="low_sum")
-                nc.tensor.matmul(low_sum[:], plus[:], low_cos[:], start=True, stop=False)
-                nc.tensor.matmul(low_sum[:], minus[:], high_sin[:], start=False, stop=True)
-                low_out = work.tile([P, PIECE], F32, name="low_out")
-                nc.scalar.copy(low_out[:], low_sum[:])
-                nc.sync.dma_start(out[a * P : (a + 1) * P, cols], low_out[:])
-
-                high_cos = work.tile([P, PIECE], F32, name="high_cos")
-                nc.vector.tensor_tensor(high_cos[:], high[:].indirect(picks), cosines[a][:, cols], MULT)
-                low_sin = work.tile([P, PIECE], F32, name="low_sin")
-                nc.vector.tensor_tensor(low_sin[:], low[:].indirect(picks), sines[a][:, cols], MULT)
-                high_sum = sums.tile([P, PIECE], F32, name="high_sum")
-                nc.tensor.matmul(high_sum[:], plus[:], high_cos[:], start=True, stop=False)
-                nc.tensor.matmul(high_sum[:], plus[:], low_sin[:], start=False, stop=True)
-                high_out = work.tile([P, PIECE], F32, name="high_out")
-                nc.scalar.copy(high_out[:], high_sum[:])
-                nc.sync.dma_start(out[(a + AXES) * P : (a + AXES + 1) * P, cols], high_out[:])
+                for b, partner, sign in ((a, a + AXES, minus), (a + AXES, a, plus)):
+                    by_cos = work.tile([P, PIECE], F32, name="by_cos")
+                    nc.vector.tensor_tensor(by_cos[:], words[b][:].indirect(picks), cosine[:, cols], MULT)
+                    by_sin = work.tile([P, PIECE], F32, name="by_sin")
+                    nc.vector.tensor_tensor(by_sin[:], words[partner][:].indirect(picks), sine[:, cols], MULT)
+                    turned = work.tile([P, PIECE], F32, name="turned")
+                    if (b, start) == last_sum:
+                        nc.vector.tensor_tensor(turned[:], by_cos[:], by_sin[:], ADD)
+                    else:
+                        total = sums.tile([P, PIECE], F32, name="total")
+                        nc.tensor.matmul(total[:], plus[:], by_cos[:], start=True, stop=False)
+                        nc.tensor.matmul(total[:], sign[:], by_sin[:], start=False, stop=True)
+                        nc.scalar.copy(turned[:], total[:])
+                    nc.sync.dma_start(out[b * P : (b + 1) * P, cols], turned[:])

@@ -47,7 +47,8 @@ def tile_arcembedding_kernel(tc, table, pos, freq, offs, out):
         places = [held.tile([P, TOKENS], F32, name=f"place{a}") for a in range(AXES)]
         words = [held.tile([P, WORDS], F32, name=f"words{b}") for b in range(2 * AXES)]
         for a in range(AXES):
-            nc.sync.dma_start(places[a][:], pos[a, :].partition_broadcast(P))
+            queue = nc.scalar if a == 1 else nc.sync
+            queue.dma_start(places[a][:], pos[a, :].partition_broadcast(P))
             for b in (a, a + AXES):
                 nc.sync.dma_start(words[b][:], table[b * P : (b + 1) * P, :])
 
@@ -72,10 +73,10 @@ def tile_arcembedding_kernel(tc, table, pos, freq, offs, out):
         last_sum = (2 * AXES - 1, TOKENS - PIECE)
         turns = [cosine_and_sine(nc, held, places[0], pitch, quarter_turn, 0)]
         for a in range(AXES):
+            if a + 1 < AXES:
+                turns.append(cosine_and_sine(nc, held, places[a + 1], pitch, quarter_turn, a + 1))
             cosine, sine = turns[a]
             for start in range(0, TOKENS, PIECE):
-                if start == PIECE and a + 1 < AXES:
-                    turns.append(cosine_and_sine(nc, held, places[a + 1], pitch, quarter_turn, a + 1))
                 cols = slice(start, start + PIECE)
                 picks = offsets[:, start // PER_COLUMN : (start + PIECE) // PER_COLUMN]
                 for b, partner, sign in ((a, a + AXES, minus), (a + AXES, a, plus)):

@@ -40,17 +40,23 @@ def tile_arcembedding_kernel(tc, table, pos, freq, offs, out):
         tc.tile_pool(name="work", bufs=6) as work,
         tc.psum_pool(name="sums", bufs=6) as sums,
     ):
-        offsets = held.tile([P, TOKENS // PER_COLUMN], U16, name="offsets")
-        nc.sync.dma_start(offsets[:], offs)
         pitch = held.tile([P, 1], F32, name="pitch")
         nc.scalar.dma_start(pitch[:], freq)
+        offsets = held.tile([P, TOKENS // PER_COLUMN], U16, name="offsets")
         places = [held.tile([P, TOKENS], F32, name=f"place{a}") for a in range(AXES)]
         words = [held.tile([P, WORDS], F32, name=f"words{b}") for b in range(2 * AXES)]
         for a in range(AXES):
             queue = nc.scalar if a == 1 else nc.sync
             queue.dma_start(places[a][:], pos[a, :].partition_broadcast(P))
+            if a == 0:
+                nc.sync.dma_start(offsets[:], offs)
             for b in (a, a + AXES):
                 nc.sync.dma_start(words[b][:], table[b * P : (b + 1) * P, :])
+
+        quarter_turn = held.tile([P, 1], F32, name="quarter_turn")
+        nc.gpsimd.memset(quarter_turn[:], math.pi / 2)
+        first_sine = held.tile([P, 1], F32, name="first_sine")
+        nc.scalar.activation(first_sine[:], quarter_turn[:], SIN)
 
         plus = held.tile([P, P], F32, name="plus")
         make_identity(nc, plus[:])
@@ -65,10 +71,6 @@ def tile_arcembedding_kernel(tc, table, pos, freq, offs, out):
             pattern=[[-1, P]],
             channel_multiplier=1,
         )
-        quarter_turn = held.tile([P, 1], F32, name="quarter_turn")
-        nc.vector.memset(quarter_turn[:], math.pi / 2)
-        first_sine = held.tile([P, 1], F32, name="first_sine")
-        nc.scalar.activation(first_sine[:], quarter_turn[:], SIN)
 
         last_sum = (2 * AXES - 1, TOKENS - PIECE)
         turns = [cosine_and_sine(nc, held, places[0], pitch, quarter_turn, 0)]

@@ -9,6 +9,7 @@ MULT = mybir.AluOpType.mult
 ADD = mybir.AluOpType.add
 MAX = mybir.AluOpType.max
 SIN = mybir.ActivationFunctionType.Sin
+COPY = mybir.ActivationFunctionType.Copy
 
 P = 128
 WORDS = 256
@@ -21,9 +22,10 @@ PER_COLUMN = 16
 def cosine_and_sine(nc, pool, place, pitch, quarter_turn, a):
     top = pool.tile([P, 1], F32, name=f"top{a}")
     nc.vector.tensor_reduce(top[:], place[:], mybir.AxisListType.X, MAX)
+    inverse = pool.tile([P, 1], F32, name=f"inverse{a}")
+    nc.vector.reciprocal(inverse[:], top[:])
     rate = pool.tile([P, 1], F32, name=f"rate{a}")
-    nc.vector.reciprocal(rate[:], top[:])
-    nc.vector.tensor_tensor(rate[:], rate[:], pitch[:], MULT)
+    nc.scalar.activation(rate[:], inverse[:], COPY, scale=pitch[:])
     cosine = pool.tile([P, TOKENS], F32, name=f"cosine{a}")
     sine = pool.tile([P, TOKENS], F32, name=f"sine{a}")
     for start in range(0, TOKENS, PIECE):
@@ -40,23 +42,17 @@ def tile_arcembedding_kernel(tc, table, pos, freq, offs, out):
         tc.tile_pool(name="work", bufs=6) as work,
         tc.psum_pool(name="sums", bufs=6) as sums,
     ):
+        offsets = held.tile([P, TOKENS // PER_COLUMN], U16, name="offsets")
+        nc.sync.dma_start(offsets[:], offs)
         pitch = held.tile([P, 1], F32, name="pitch")
         nc.scalar.dma_start(pitch[:], freq)
-        offsets = held.tile([P, TOKENS // PER_COLUMN], U16, name="offsets")
         places = [held.tile([P, TOKENS], F32, name=f"place{a}") for a in range(AXES)]
         words = [held.tile([P, WORDS], F32, name=f"words{b}") for b in range(2 * AXES)]
         for a in range(AXES):
             queue = nc.scalar if a == 1 else nc.sync
             queue.dma_start(places[a][:], pos[a, :].partition_broadcast(P))
-            if a == 0:
-                nc.sync.dma_start(offsets[:], offs)
             for b in (a, a + AXES):
                 nc.sync.dma_start(words[b][:], table[b * P : (b + 1) * P, :])
-
-        quarter_turn = held.tile([P, 1], F32, name="quarter_turn")
-        nc.gpsimd.memset(quarter_turn[:], math.pi / 2)
-        first_sine = held.tile([P, 1], F32, name="first_sine")
-        nc.scalar.activation(first_sine[:], quarter_turn[:], SIN)
 
         plus = held.tile([P, P], F32, name="plus")
         make_identity(nc, plus[:])
@@ -71,6 +67,10 @@ def tile_arcembedding_kernel(tc, table, pos, freq, offs, out):
             pattern=[[-1, P]],
             channel_multiplier=1,
         )
+        quarter_turn = held.tile([P, 1], F32, name="quarter_turn")
+        nc.vector.memset(quarter_turn[:], math.pi / 2)
+        first_sine = held.tile([P, 1], F32, name="first_sine")
+        nc.scalar.activation(first_sine[:], quarter_turn[:], SIN)
 
         last_sum = (2 * AXES - 1, TOKENS - PIECE)
         turns = [cosine_and_sine(nc, held, places[0], pitch, quarter_turn, 0)]

@@ -9,7 +9,6 @@ MULT = mybir.AluOpType.mult
 ADD = mybir.AluOpType.add
 MAX = mybir.AluOpType.max
 SIN = mybir.ActivationFunctionType.Sin
-COPY = mybir.ActivationFunctionType.Copy
 
 P = 128
 WORDS = 256
@@ -22,10 +21,9 @@ PER_COLUMN = 16
 def cosine_and_sine(nc, pool, place, pitch, quarter_turn, a):
     top = pool.tile([P, 1], F32, name=f"top{a}")
     nc.vector.tensor_reduce(top[:], place[:], mybir.AxisListType.X, MAX)
-    inverse = pool.tile([P, 1], F32, name=f"inverse{a}")
-    nc.vector.reciprocal(inverse[:], top[:])
     rate = pool.tile([P, 1], F32, name=f"rate{a}")
-    nc.scalar.activation(rate[:], inverse[:], COPY, scale=pitch[:])
+    nc.vector.reciprocal(rate[:], top[:])
+    nc.vector.tensor_tensor(rate[:], rate[:], pitch[:], MULT)
     cosine = pool.tile([P, TOKENS], F32, name=f"cosine{a}")
     sine = pool.tile([P, TOKENS], F32, name=f"sine{a}")
     for start in range(0, TOKENS, PIECE):
@@ -42,15 +40,16 @@ def tile_arcembedding_kernel(tc, table, pos, freq, offs, out):
         tc.tile_pool(name="work", bufs=6) as work,
         tc.psum_pool(name="sums", bufs=6) as sums,
     ):
-        offsets = held.tile([P, TOKENS // PER_COLUMN], U16, name="offsets")
-        nc.sync.dma_start(offsets[:], offs)
         pitch = held.tile([P, 1], F32, name="pitch")
         nc.scalar.dma_start(pitch[:], freq)
+        offsets = held.tile([P, TOKENS // PER_COLUMN], U16, name="offsets")
         places = [held.tile([P, TOKENS], F32, name=f"place{a}") for a in range(AXES)]
         words = [held.tile([P, WORDS], F32, name=f"words{b}") for b in range(2 * AXES)]
         for a in range(AXES):
             queue = nc.scalar if a == 1 else nc.sync
             queue.dma_start(places[a][:], pos[a, :].partition_broadcast(P))
+            if a == 0:
+                nc.sync.dma_start(offsets[:], offs)
             for b in (a, a + AXES):
                 nc.sync.dma_start(words[b][:], table[b * P : (b + 1) * P, :])
 

@@ -16,6 +16,7 @@ TOKENS = 512
 AXES = 3
 PIECE = 256
 PER_COLUMN = 16
+IN_FLIGHT = 6
 
 
 def cosine_and_sine(nc, pool, place, pitch, quarter_turn, a):
@@ -37,19 +38,18 @@ def tile_arcembedding_kernel(tc, table, pos, freq, offs, out):
     nc = tc.nc
     with (
         tc.tile_pool(name="held", bufs=1) as held,
-        tc.tile_pool(name="work", bufs=6) as work,
-        tc.psum_pool(name="sums", bufs=6) as sums,
+        tc.tile_pool(name="work", bufs=IN_FLIGHT) as work,
+        tc.psum_pool(name="sums", bufs=IN_FLIGHT) as sums,
     ):
-        pitch = held.tile([P, 1], F32, name="pitch")
-        nc.scalar.dma_start(pitch[:], freq)
         offsets = held.tile([P, TOKENS // PER_COLUMN], U16, name="offsets")
+        nc.sync.dma_start(offsets[:], offs)
+        pitch = held.tile([P, 1], F32, name="pitch")
+        nc.sync.dma_start(pitch[:], freq)
         places = [held.tile([P, TOKENS], F32, name=f"place{a}") for a in range(AXES)]
         words = [held.tile([P, WORDS], F32, name=f"words{b}") for b in range(2 * AXES)]
         for a in range(AXES):
-            queue = nc.scalar if a == 1 else nc.sync
+            queue = nc.scalar if a == 0 else nc.sync
             queue.dma_start(places[a][:], pos[a, :].partition_broadcast(P))
-            if a == 0:
-                nc.sync.dma_start(offsets[:], offs)
             for b in (a, a + AXES):
                 nc.sync.dma_start(words[b][:], table[b * P : (b + 1) * P, :])
 
@@ -80,7 +80,7 @@ def tile_arcembedding_kernel(tc, table, pos, freq, offs, out):
             for start in range(0, TOKENS, PIECE):
                 cols = slice(start, start + PIECE)
                 picks = offsets[:, start // PER_COLUMN : (start + PIECE) // PER_COLUMN]
-                for b, partner, sign in ((a, a + AXES, minus), (a + AXES, a, plus)):
+                for b, partner, signed_unit in ((a, a + AXES, minus), (a + AXES, a, plus)):
                     by_cos = work.tile([P, PIECE], F32, name="by_cos")
                     nc.vector.tensor_tensor(by_cos[:], words[b][:].indirect(picks), cosine[:, cols], MULT)
                     by_sin = work.tile([P, PIECE], F32, name="by_sin")
@@ -91,6 +91,6 @@ def tile_arcembedding_kernel(tc, table, pos, freq, offs, out):
                     else:
                         total = sums.tile([P, PIECE], F32, name="total")
                         nc.tensor.matmul(total[:], plus[:], by_cos[:], start=True, stop=False)
-                        nc.tensor.matmul(total[:], sign[:], by_sin[:], start=False, stop=True)
+                        nc.tensor.matmul(total[:], signed_unit[:], by_sin[:], start=False, stop=True)
                         nc.scalar.copy(turned[:], total[:])
                     nc.sync.dma_start(out[b * P : (b + 1) * P, cols], turned[:])

@@ -9,6 +9,7 @@ MULT = mybir.AluOpType.mult
 ADD = mybir.AluOpType.add
 MAX = mybir.AluOpType.max
 SIN = mybir.ActivationFunctionType.Sin
+COPY = mybir.ActivationFunctionType.Copy
 
 P = 128
 WORDS = 256
@@ -19,18 +20,13 @@ PER_COLUMN = 16
 IN_FLIGHT = 6
 
 
-def cosine_and_sine(nc, pool, place, pitch, quarter_turn, a):
-    top = pool.tile([P, 1], F32, name=f"top{a}")
-    nc.vector.tensor_reduce(top[:], place[:], mybir.AxisListType.X, MAX)
-    rate = pool.tile([P, 1], F32, name=f"rate{a}")
-    nc.vector.reciprocal(rate[:], top[:])
-    nc.vector.tensor_tensor(rate[:], rate[:], pitch[:], MULT)
+def cosine_and_sine(nc, pool, place, rate, quarter_turn, a):
     cosine = pool.tile([P, TOKENS], F32, name=f"cosine{a}")
     sine = pool.tile([P, TOKENS], F32, name=f"sine{a}")
     for start in range(0, TOKENS, PIECE):
         cols = slice(start, start + PIECE)
-        nc.scalar.activation(cosine[:, cols], place[:, cols], SIN, bias=quarter_turn[:], scale=rate[:])
-        nc.scalar.activation(sine[:, cols], place[:, cols], SIN, scale=rate[:])
+        nc.scalar.activation(cosine[:, cols], place[:, cols], SIN, bias=quarter_turn[:], scale=rate)
+        nc.scalar.activation(sine[:, cols], place[:, cols], SIN, scale=rate)
     return cosine, sine
 
 
@@ -40,11 +36,14 @@ def tile_arcembedding_kernel(tc, table, pos, freq, offs, out):
         tc.tile_pool(name="held", bufs=1) as held,
         tc.tile_pool(name="work", bufs=IN_FLIGHT) as work,
         tc.psum_pool(name="sums", bufs=IN_FLIGHT) as sums,
+        tc.psum_pool(name="once", bufs=1) as once,
     ):
         offsets = held.tile([P, TOKENS // PER_COLUMN], U16, name="offsets")
         nc.sync.dma_start(offsets[:], offs)
         pitch = held.tile([P, 1], F32, name="pitch")
         nc.sync.dma_start(pitch[:], freq)
+        later_rows = held.tile([AXES - 1, TOKENS], F32, name="later_rows")
+        nc.sync.dma_start(later_rows[:], pos[1:AXES, :])
         places = [held.tile([P, TOKENS], F32, name=f"place{a}") for a in range(AXES)]
         words = [held.tile([P, WORDS], F32, name=f"words{b}") for b in range(2 * AXES)]
         for a in range(AXES):
@@ -53,6 +52,17 @@ def tile_arcembedding_kernel(tc, table, pos, freq, offs, out):
             for b in (a, a + AXES):
                 nc.sync.dma_start(words[b][:], table[b * P : (b + 1) * P, :])
 
+        selector = held.tile([AXES - 1, (AXES - 1) * P], F32, name="selector")
+        nc.gpsimd.memset(selector[:], 0.0)
+        nc.gpsimd.affine_select(
+            out=selector[:],
+            in_=selector[:],
+            compare_op=mybir.AluOpType.not_equal,
+            fill=1.0,
+            base=0,
+            pattern=[[-1, AXES - 1], [0, P]],
+            channel_multiplier=1,
+        )
         plus = held.tile([P, P], F32, name="plus")
         make_identity(nc, plus[:])
         minus = held.tile([P, P], F32, name="minus")
@@ -71,11 +81,26 @@ def tile_arcembedding_kernel(tc, table, pos, freq, offs, out):
         first_sine = held.tile([P, 1], F32, name="first_sine")
         nc.scalar.activation(first_sine[:], quarter_turn[:], SIN)
 
+        rates = held.tile([P, AXES], F32, name="rates")
+        top = held.tile([P, 1], F32, name="top")
+        nc.vector.tensor_reduce(top[:], places[0][:], mybir.AxisListType.X, MAX)
+        inverse = held.tile([P, 1], F32, name="inverse")
+        nc.vector.reciprocal(inverse[:], top[:])
+        nc.vector.tensor_tensor(rates[:, 0:1], inverse[:], pitch[:], MULT)
+        later_tops = held.tile([AXES - 1, 1], F32, name="later_tops")
+        nc.vector.tensor_reduce(later_tops[:], later_rows[:], mybir.AxisListType.X, MAX)
+        later_inverses = held.tile([AXES - 1, 1], F32, name="later_inverses")
+        nc.vector.reciprocal(later_inverses[:], later_tops[:])
+        spread = once.tile([P, AXES - 1], F32, name="spread")
+        for i in range(AXES - 1):
+            nc.tensor.matmul(spread[:, i : i + 1], selector[:, i * P : (i + 1) * P], later_inverses[:], start=True, stop=True)
+
         last_sum = (2 * AXES - 1, TOKENS - PIECE)
-        turns = [cosine_and_sine(nc, held, places[0], pitch, quarter_turn, 0)]
+        turns = [cosine_and_sine(nc, held, places[0], rates[:, 0:1], quarter_turn, 0)]
+        nc.scalar.activation(rates[:, 1:AXES], spread[:], COPY, scale=pitch[:])
         for a in range(AXES):
             if a + 1 < AXES:
-                turns.append(cosine_and_sine(nc, held, places[a + 1], pitch, quarter_turn, a + 1))
+                turns.append(cosine_and_sine(nc, held, places[a + 1], rates[:, a + 1 : a + 2], quarter_turn, a + 1))
             cosine, sine = turns[a]
             for start in range(0, TOKENS, PIECE):
                 cols = slice(start, start + PIECE)

@@ -81,12 +81,12 @@ def tile_arcembedding_kernel(tc, table, pos, freq, offs, out):
         first_sine = held.tile([P, 1], F32, name="first_sine")
         nc.scalar.activation(first_sine[:], quarter_turn[:], SIN)
 
-        rates = held.tile([P, AXES], F32, name="rates")
         top = held.tile([P, 1], F32, name="top")
         nc.vector.tensor_reduce(top[:], places[0][:], mybir.AxisListType.X, MAX)
         inverse = held.tile([P, 1], F32, name="inverse")
         nc.vector.reciprocal(inverse[:], top[:])
-        nc.vector.tensor_tensor(rates[:, 0:1], inverse[:], pitch[:], MULT)
+        pitched = held.tile([P, TOKENS], F32, name="pitched")
+        nc.scalar.activation(pitched[:], places[0][:], COPY, scale=pitch[:])
         later_tops = held.tile([AXES - 1, 1], F32, name="later_tops")
         nc.vector.tensor_reduce(later_tops[:], later_rows[:], mybir.AxisListType.X, MAX)
         later_inverses = held.tile([AXES - 1, 1], F32, name="later_inverses")
@@ -96,11 +96,12 @@ def tile_arcembedding_kernel(tc, table, pos, freq, offs, out):
             nc.tensor.matmul(spread[:, i : i + 1], selector[:, i * P : (i + 1) * P], later_inverses[:], start=True, stop=True)
 
         last_sum = (2 * AXES - 1, TOKENS - PIECE)
-        turns = [cosine_and_sine(nc, held, places[0], rates[:, 0:1], quarter_turn, 0)]
-        nc.scalar.activation(rates[:, 1:AXES], spread[:], COPY, scale=pitch[:])
+        turns = [cosine_and_sine(nc, held, pitched, inverse[:], quarter_turn, 0)]
+        later_rates = held.tile([P, AXES - 1], F32, name="later_rates")
+        nc.scalar.activation(later_rates[:], spread[:], COPY, scale=pitch[:])
         for a in range(AXES):
             if a + 1 < AXES:
-                turns.append(cosine_and_sine(nc, held, places[a + 1], rates[:, a + 1 : a + 2], quarter_turn, a + 1))
+                turns.append(cosine_and_sine(nc, held, places[a + 1], later_rates[:, a : a + 1], quarter_turn, a + 1))
             cosine, sine = turns[a]
             for start in range(0, TOKENS, PIECE):
                 cols = slice(start, start + PIECE)

@@ -38,12 +38,12 @@ def tile_arcembedding_kernel(tc, table, pos, freq, offs, out):
         tc.psum_pool(name="sums", bufs=IN_FLIGHT) as sums,
         tc.psum_pool(name="once", bufs=1) as once,
     ):
-        offsets = held.tile([P, TOKENS // PER_COLUMN], U16, name="offsets")
-        nc.sync.dma_start(offsets[:], offs)
         pitch = held.tile([P, 1], F32, name="pitch")
         nc.sync.dma_start(pitch[:], freq)
         later_rows = held.tile([AXES - 1, TOKENS], F32, name="later_rows")
         nc.sync.dma_start(later_rows[:], pos[1:AXES, :])
+        offsets = held.tile([P, TOKENS // PER_COLUMN], U16, name="offsets")
+        nc.sync.dma_start(offsets[:], offs)
         places = [held.tile([P, TOKENS], F32, name=f"place{a}") for a in range(AXES)]
         words = [held.tile([P, WORDS], F32, name=f"words{b}") for b in range(2 * AXES)]
         for a in range(AXES):

@@ -17,6 +17,7 @@ TOKENS = 512
 AXES = 3
 PIECE = 256
 PER_COLUMN = 16
+SUMS = 2 * AXES * (TOKENS // PIECE)
 IN_FLIGHT = 6
 
 
@@ -34,7 +35,7 @@ def tile_arcembedding_kernel(tc, table, pos, freq, offs, out):
     nc = tc.nc
     with (
         tc.tile_pool(name="held", bufs=1) as held,
-        tc.tile_pool(name="work", bufs=IN_FLIGHT) as work,
+        tc.tile_pool(name="work", bufs=SUMS) as work,
         tc.psum_pool(name="sums", bufs=IN_FLIGHT) as sums,
         tc.psum_pool(name="once", bufs=1) as once,
     ):

@@ -7,6 +7,7 @@ F32 = mybir.dt.float32
 U16 = mybir.dt.uint16
 MULT = mybir.AluOpType.mult
 ADD = mybir.AluOpType.add
+SUBTRACT = mybir.AluOpType.subtract
 MAX = mybir.AluOpType.max
 SIN = mybir.ActivationFunctionType.Sin
 COPY = mybir.ActivationFunctionType.Copy
@@ -96,7 +97,7 @@ def tile_arcembedding_kernel(tc, table, pos, freq, offs, out):
         for i in range(AXES - 1):
             nc.tensor.matmul(spread[:, i : i + 1], selector[:, i * P : (i + 1) * P], later_inverses[:], start=True, stop=True)
 
-        last_sum = (2 * AXES - 1, TOKENS - PIECE)
+        last_piece = (AXES - 1, TOKENS - PIECE)
         turns = [cosine_and_sine(nc, held, pitched, inverse[:], quarter_turn, 0)]
         later_rates = held.tile([P, AXES - 1], F32, name="later_rates")
         nc.scalar.activation(later_rates[:], spread[:], COPY, scale=pitch[:])
@@ -107,14 +108,19 @@ def tile_arcembedding_kernel(tc, table, pos, freq, offs, out):
             for start in range(0, TOKENS, PIECE):
                 cols = slice(start, start + PIECE)
                 picks = offsets[:, start // PER_COLUMN : (start + PIECE) // PER_COLUMN]
-                for b, partner, signed_unit in ((a, a + AXES, minus), (a + AXES, a, plus)):
+                products = []
+                for b, partner in ((a, a + AXES), (a + AXES, a)):
                     by_cos = work.tile([P, PIECE], F32, name="by_cos")
                     nc.vector.tensor_tensor(by_cos[:], words[b][:].indirect(picks), cosine[:, cols], MULT)
                     by_sin = work.tile([P, PIECE], F32, name="by_sin")
                     nc.vector.tensor_tensor(by_sin[:], words[partner][:].indirect(picks), sine[:, cols], MULT)
+                    products.append((by_cos, by_sin))
+                for (by_cos, by_sin), b, signed_unit, signed_op in zip(
+                    products, (a, a + AXES), (minus, plus), (SUBTRACT, ADD)
+                ):
                     turned = work.tile([P, PIECE], F32, name="turned")
-                    if (b, start) == last_sum:
-                        nc.vector.tensor_tensor(turned[:], by_cos[:], by_sin[:], ADD)
+                    if (a, start) == last_piece:
+                        nc.vector.tensor_tensor(turned[:], by_cos[:], by_sin[:], signed_op)
                     else:
                         total = sums.tile([P, PIECE], F32, name="total")
                         nc.tensor.matmul(total[:], plus[:], by_cos[:], start=True, stop=False)

@@ -16,6 +16,9 @@ P = 128
 WORDS = 256
 TOKENS = 512
 AXES = 3
+GRID_AXES = 2
+SEQUENCE = 2
+ORDER = (SEQUENCE, 0, 1)
 PIECE = 256
 PER_COLUMN = 16
 SUMS = 2 * AXES * (TOKENS // PIECE)
@@ -42,19 +45,19 @@ def tile_arcembedding_kernel(tc, table, pos, freq, offs, out):
     ):
         pitch = held.tile([P, 1], F32, name="pitch")
         nc.sync.dma_start(pitch[:], freq)
-        later_rows = held.tile([AXES - 1, TOKENS], F32, name="later_rows")
-        nc.sync.dma_start(later_rows[:], pos[1:AXES, :])
         offsets = held.tile([P, TOKENS // PER_COLUMN], U16, name="offsets")
         nc.sync.dma_start(offsets[:], offs)
+        grid_rows = held.tile([GRID_AXES, TOKENS], F32, name="grid_rows")
+        nc.sync.dma_start(grid_rows[:], pos[0:GRID_AXES, :])
         places = [held.tile([P, TOKENS], F32, name=f"place{a}") for a in range(AXES)]
         words = [held.tile([P, WORDS], F32, name=f"words{b}") for b in range(2 * AXES)]
-        for a in range(AXES):
-            queue = nc.scalar if a == 0 else nc.sync
+        for a in ORDER:
+            queue = nc.scalar if a == SEQUENCE else nc.sync
             queue.dma_start(places[a][:], pos[a, :].partition_broadcast(P))
             for b in (a, a + AXES):
                 nc.sync.dma_start(words[b][:], table[b * P : (b + 1) * P, :])
 
-        selector = held.tile([AXES - 1, (AXES - 1) * P], F32, name="selector")
+        selector = held.tile([GRID_AXES, GRID_AXES * P], F32, name="selector")
         nc.gpsimd.memset(selector[:], 0.0)
         nc.gpsimd.affine_select(
             out=selector[:],
@@ -62,7 +65,7 @@ def tile_arcembedding_kernel(tc, table, pos, freq, offs, out):
             compare_op=mybir.AluOpType.not_equal,
             fill=1.0,
             base=0,
-            pattern=[[-1, AXES - 1], [0, P]],
+            pattern=[[-1, GRID_AXES], [0, P]],
             channel_multiplier=1,
         )
         plus = held.tile([P, P], F32, name="plus")
@@ -83,27 +86,27 @@ def tile_arcembedding_kernel(tc, table, pos, freq, offs, out):
         first_sine = held.tile([P, 1], F32, name="first_sine")
         nc.scalar.activation(first_sine[:], quarter_turn[:], SIN)
 
-        top = held.tile([P, 1], F32, name="top")
-        nc.vector.tensor_reduce(top[:], places[0][:], mybir.AxisListType.X, MAX)
         inverse = held.tile([P, 1], F32, name="inverse")
-        nc.vector.reciprocal(inverse[:], top[:])
+        nc.vector.reciprocal(inverse[:], places[SEQUENCE][:, TOKENS - 1 : TOKENS])
         pitched = held.tile([P, TOKENS], F32, name="pitched")
-        nc.scalar.activation(pitched[:], places[0][:], COPY, scale=pitch[:])
-        later_tops = held.tile([AXES - 1, 1], F32, name="later_tops")
-        nc.vector.tensor_reduce(later_tops[:], later_rows[:], mybir.AxisListType.X, MAX)
-        later_inverses = held.tile([AXES - 1, 1], F32, name="later_inverses")
-        nc.vector.reciprocal(later_inverses[:], later_tops[:])
-        spread = once.tile([P, AXES - 1], F32, name="spread")
-        for i in range(AXES - 1):
-            nc.tensor.matmul(spread[:, i : i + 1], selector[:, i * P : (i + 1) * P], later_inverses[:], start=True, stop=True)
+        nc.scalar.activation(pitched[:], places[SEQUENCE][:], COPY, scale=pitch[:])
+        grid_tops = held.tile([GRID_AXES, 1], F32, name="grid_tops")
+        nc.vector.tensor_reduce(grid_tops[:], grid_rows[:], mybir.AxisListType.X, MAX)
+        grid_inverses = held.tile([GRID_AXES, 1], F32, name="grid_inverses")
+        nc.vector.reciprocal(grid_inverses[:], grid_tops[:])
+        spread = once.tile([P, GRID_AXES], F32, name="spread")
+        for a in range(GRID_AXES):
+            nc.tensor.matmul(spread[:, a : a + 1], selector[:, a * P : (a + 1) * P], grid_inverses[:], start=True, stop=True)
 
-        last_piece = (AXES - 1, TOKENS - PIECE)
-        turns = [cosine_and_sine(nc, held, pitched, inverse[:], quarter_turn, 0)]
-        later_rates = held.tile([P, AXES - 1], F32, name="later_rates")
-        nc.scalar.activation(later_rates[:], spread[:], COPY, scale=pitch[:])
-        for a in range(AXES):
-            if a + 1 < AXES:
-                turns.append(cosine_and_sine(nc, held, places[a + 1], later_rates[:, a : a + 1], quarter_turn, a + 1))
+        last_piece = (ORDER[-1], TOKENS - PIECE)
+        turns = {SEQUENCE: cosine_and_sine(nc, held, pitched, inverse[:], quarter_turn, SEQUENCE)}
+        grid_rates = held.tile([P, GRID_AXES], F32, name="grid_rates")
+        nc.scalar.activation(grid_rates[:], spread[:], COPY, scale=pitch[:])
+        for a, following in zip(ORDER, ORDER[1:] + (None,)):
+            if following is not None:
+                turns[following] = cosine_and_sine(
+                    nc, held, places[following], grid_rates[:, following : following + 1], quarter_turn, following
+                )
             cosine, sine = turns[a]
             for start in range(0, TOKENS, PIECE):
                 cols = slice(start, start + PIECE)

@@ -20,15 +20,16 @@ GRID_AXES = 2
 SEQUENCE = 2
 ORDER = (SEQUENCE, 0, 1)
 PIECE = 256
+STARTS = (TOKENS - PIECE, 0)
 PER_COLUMN = 16
-SUMS = 2 * AXES * (TOKENS // PIECE)
+PIECES = AXES * len(STARTS)
 IN_FLIGHT = 6
 
 
 def cosine_and_sine(nc, pool, place, rate, quarter_turn, a):
     cosine = pool.tile([P, TOKENS], F32, name=f"cosine{a}")
     sine = pool.tile([P, TOKENS], F32, name=f"sine{a}")
-    for start in range(0, TOKENS, PIECE):
+    for start in STARTS:
         cols = slice(start, start + PIECE)
         nc.scalar.activation(cosine[:, cols], place[:, cols], SIN, bias=quarter_turn[:], scale=rate)
         nc.scalar.activation(sine[:, cols], place[:, cols], SIN, scale=rate)
@@ -39,7 +40,7 @@ def tile_arcembedding_kernel(tc, table, pos, freq, offs, out):
     nc = tc.nc
     with (
         tc.tile_pool(name="held", bufs=1) as held,
-        tc.tile_pool(name="work", bufs=SUMS) as work,
+        tc.tile_pool(name="work", bufs=PIECES) as work,
         tc.psum_pool(name="sums", bufs=IN_FLIGHT) as sums,
         tc.psum_pool(name="once", bufs=1) as once,
     ):
@@ -47,13 +48,17 @@ def tile_arcembedding_kernel(tc, table, pos, freq, offs, out):
         nc.sync.dma_start(pitch[:], freq)
         offsets = held.tile([P, TOKENS // PER_COLUMN], U16, name="offsets")
         nc.sync.dma_start(offsets[:], offs)
-        grid_rows = held.tile([GRID_AXES, TOKENS], F32, name="grid_rows")
-        nc.sync.dma_start(grid_rows[:], pos[0:GRID_AXES, :])
         places = [held.tile([P, TOKENS], F32, name=f"place{a}") for a in range(AXES)]
         words = [held.tile([P, WORDS], F32, name=f"words{b}") for b in range(2 * AXES)]
-        for a in ORDER:
-            queue = nc.scalar if a == SEQUENCE else nc.sync
-            queue.dma_start(places[a][:], pos[a, :].partition_broadcast(P))
+        for start in STARTS:
+            cols = slice(start, start + PIECE)
+            nc.scalar.dma_start(places[SEQUENCE][:, cols], pos[SEQUENCE, cols].partition_broadcast(P))
+        for b in (SEQUENCE, SEQUENCE + AXES):
+            nc.sync.dma_start(words[b][:], table[b * P : (b + 1) * P, :])
+        grid_rows = held.tile([GRID_AXES, TOKENS], F32, name="grid_rows")
+        nc.sync.dma_start(grid_rows[:], pos[0:GRID_AXES, :])
+        for a in range(GRID_AXES):
+            nc.sync.dma_start(places[a][:], pos[a, :].partition_broadcast(P))
             for b in (a, a + AXES):
                 nc.sync.dma_start(words[b][:], table[b * P : (b + 1) * P, :])
 
@@ -89,7 +94,9 @@ def tile_arcembedding_kernel(tc, table, pos, freq, offs, out):
         inverse = held.tile([P, 1], F32, name="inverse")
         nc.vector.reciprocal(inverse[:], places[SEQUENCE][:, TOKENS - 1 : TOKENS])
         pitched = held.tile([P, TOKENS], F32, name="pitched")
-        nc.scalar.activation(pitched[:], places[SEQUENCE][:], COPY, scale=pitch[:])
+        for start in STARTS:
+            cols = slice(start, start + PIECE)
+            nc.scalar.activation(pitched[:, cols], places[SEQUENCE][:, cols], COPY, scale=pitch[:])
         grid_tops = held.tile([GRID_AXES, 1], F32, name="grid_tops")
         nc.vector.tensor_reduce(grid_tops[:], grid_rows[:], mybir.AxisListType.X, MAX)
         grid_inverses = held.tile([GRID_AXES, 1], F32, name="grid_inverses")
@@ -98,7 +105,7 @@ def tile_arcembedding_kernel(tc, table, pos, freq, offs, out):
         for a in range(GRID_AXES):
             nc.tensor.matmul(spread[:, a : a + 1], selector[:, a * P : (a + 1) * P], grid_inverses[:], start=True, stop=True)
 
-        last_piece = (ORDER[-1], TOKENS - PIECE)
+        last_piece = (ORDER[-1], STARTS[-1])
         turns = {SEQUENCE: cosine_and_sine(nc, held, pitched, inverse[:], quarter_turn, SEQUENCE)}
         grid_rates = held.tile([P, GRID_AXES], F32, name="grid_rates")
         nc.scalar.activation(grid_rates[:], spread[:], COPY, scale=pitch[:])
@@ -108,25 +115,28 @@ def tile_arcembedding_kernel(tc, table, pos, freq, offs, out):
                     nc, held, places[following], grid_rates[:, following : following + 1], quarter_turn, following
                 )
             cosine, sine = turns[a]
-            for start in range(0, TOKENS, PIECE):
+            low, high = a, a + AXES
+            for start in STARTS:
                 cols = slice(start, start + PIECE)
                 picks = offsets[:, start // PER_COLUMN : (start + PIECE) // PER_COLUMN]
-                products = []
-                for b, partner in ((a, a + AXES), (a + AXES, a)):
-                    by_cos = work.tile([P, PIECE], F32, name="by_cos")
-                    nc.vector.tensor_tensor(by_cos[:], words[b][:].indirect(picks), cosine[:, cols], MULT)
-                    by_sin = work.tile([P, PIECE], F32, name="by_sin")
-                    nc.vector.tensor_tensor(by_sin[:], words[partner][:].indirect(picks), sine[:, cols], MULT)
-                    products.append((by_cos, by_sin))
-                for (by_cos, by_sin), b, signed_unit, signed_op in zip(
-                    products, (a, a + AXES), (minus, plus), (SUBTRACT, ADD)
+                turned = {b: work.tile([P, PIECE], F32, name=f"turned{b // AXES}") for b in (low, high)}
+                if (a, start) != last_piece:
+                    total = {b: sums.tile([P, PIECE], F32, name="total") for b in (low, high)}
+                products = {}
+                for b, turn, target, signed_unit, first in (
+                    (low, cosine, low, plus, True),
+                    (low, sine, high, plus, True),
+                    (high, cosine, high, plus, False),
+                    (high, sine, low, minus, False),
                 ):
-                    turned = work.tile([P, PIECE], F32, name="turned")
+                    product = work.tile([P, PIECE], F32, name=f"product{len(products)}")
+                    nc.vector.tensor_tensor(product[:], words[b][:].indirect(picks), turn[:, cols], MULT)
+                    products[target, first] = product
+                    if (a, start) != last_piece:
+                        nc.tensor.matmul(total[target][:], signed_unit[:], product[:], start=first, stop=not first)
+                for b, signed_op in ((high, ADD), (low, SUBTRACT)):
                     if (a, start) == last_piece:
-                        nc.vector.tensor_tensor(turned[:], by_cos[:], by_sin[:], signed_op)
+                        nc.vector.tensor_tensor(turned[b][:], products[b, True][:], products[b, False][:], signed_op)
                     else:
-                        total = sums.tile([P, PIECE], F32, name="total")
-                        nc.tensor.matmul(total[:], plus[:], by_cos[:], start=True, stop=False)
-                        nc.tensor.matmul(total[:], signed_unit[:], by_sin[:], start=False, stop=True)
-                        nc.scalar.copy(turned[:], total[:])
-                    nc.sync.dma_start(out[b * P : (b + 1) * P, cols], turned[:])
+                        nc.scalar.copy(turned[b][:], total[b][:])
+                    nc.sync.dma_start(out[b * P : (b + 1) * P, cols], turned[b][:])

@@ -44,6 +44,8 @@ def tile_arcembedding_kernel(tc, table, pos, freq, offs, out):
         tc.psum_pool(name="sums", bufs=IN_FLIGHT) as sums,
         tc.psum_pool(name="once", bufs=1) as once,
     ):
+        grid_rows = held.tile([GRID_AXES, TOKENS], F32, name="grid_rows")
+        nc.sync.dma_start(grid_rows[:], pos[0:GRID_AXES, :])
         pitch = held.tile([P, 1], F32, name="pitch")
         nc.sync.dma_start(pitch[:], freq)
         offsets = held.tile([P, TOKENS // PER_COLUMN], U16, name="offsets")
@@ -55,8 +57,6 @@ def tile_arcembedding_kernel(tc, table, pos, freq, offs, out):
             nc.scalar.dma_start(places[SEQUENCE][:, cols], pos[SEQUENCE, cols].partition_broadcast(P))
         for b in (SEQUENCE, SEQUENCE + AXES):
             nc.sync.dma_start(words[b][:], table[b * P : (b + 1) * P, :])
-        grid_rows = held.tile([GRID_AXES, TOKENS], F32, name="grid_rows")
-        nc.sync.dma_start(grid_rows[:], pos[0:GRID_AXES, :])
         for a in range(GRID_AXES):
             nc.sync.dma_start(places[a][:], pos[a, :].partition_broadcast(P))
             for b in (a, a + AXES):
@@ -91,12 +91,6 @@ def tile_arcembedding_kernel(tc, table, pos, freq, offs, out):
         first_sine = held.tile([P, 1], F32, name="first_sine")
         nc.scalar.activation(first_sine[:], quarter_turn[:], SIN)
 
-        inverse = held.tile([P, 1], F32, name="inverse")
-        nc.vector.reciprocal(inverse[:], places[SEQUENCE][:, TOKENS - 1 : TOKENS])
-        pitched = held.tile([P, TOKENS], F32, name="pitched")
-        for start in STARTS:
-            cols = slice(start, start + PIECE)
-            nc.scalar.activation(pitched[:, cols], places[SEQUENCE][:, cols], COPY, scale=pitch[:])
         grid_tops = held.tile([GRID_AXES, 1], F32, name="grid_tops")
         nc.vector.tensor_reduce(grid_tops[:], grid_rows[:], mybir.AxisListType.X, MAX)
         grid_inverses = held.tile([GRID_AXES, 1], F32, name="grid_inverses")
@@ -104,6 +98,12 @@ def tile_arcembedding_kernel(tc, table, pos, freq, offs, out):
         spread = once.tile([P, GRID_AXES], F32, name="spread")
         for a in range(GRID_AXES):
             nc.tensor.matmul(spread[:, a : a + 1], selector[:, a * P : (a + 1) * P], grid_inverses[:], start=True, stop=True)
+        inverse = held.tile([P, 1], F32, name="inverse")
+        nc.vector.reciprocal(inverse[:], places[SEQUENCE][:, TOKENS - 1 : TOKENS])
+        pitched = held.tile([P, TOKENS], F32, name="pitched")
+        for start in STARTS:
+            cols = slice(start, start + PIECE)
+            nc.scalar.activation(pitched[:, cols], places[SEQUENCE][:, cols], COPY, scale=pitch[:])
 
         last_piece = (ORDER[-1], STARTS[-1])
         turns = {SEQUENCE: cosine_and_sine(nc, held, pitched, inverse[:], quarter_turn, SEQUENCE)}

@@ -26,14 +26,9 @@ PIECES = AXES * len(STARTS)
 IN_FLIGHT = 6
 
 
-def cosine_and_sine(nc, pool, place, rate, quarter_turn, a):
-    cosine = pool.tile([P, TOKENS], F32, name=f"cosine{a}")
-    sine = pool.tile([P, TOKENS], F32, name=f"sine{a}")
-    for start in STARTS:
-        cols = slice(start, start + PIECE)
-        nc.scalar.activation(cosine[:, cols], place[:, cols], SIN, bias=quarter_turn[:], scale=rate)
-        nc.scalar.activation(sine[:, cols], place[:, cols], SIN, scale=rate)
-    return cosine, sine
+def cosine_and_sine(nc, cosine, sine, place, rate, quarter_turn, cols):
+    nc.scalar.activation(cosine[:, cols], place[:, cols], SIN, bias=quarter_turn[:], scale=rate)
+    nc.scalar.activation(sine[:, cols], place[:, cols], SIN, scale=rate)
 
 
 def tile_arcembedding_kernel(tc, table, pos, freq, offs, out):
@@ -44,18 +39,18 @@ def tile_arcembedding_kernel(tc, table, pos, freq, offs, out):
         tc.psum_pool(name="sums", bufs=IN_FLIGHT) as sums,
         tc.psum_pool(name="once", bufs=1) as once,
     ):
-        grid_rows = held.tile([GRID_AXES, TOKENS], F32, name="grid_rows")
-        nc.sync.dma_start(grid_rows[:], pos[0:GRID_AXES, :])
         pitch = held.tile([P, 1], F32, name="pitch")
         nc.sync.dma_start(pitch[:], freq)
+        grid_rows = held.tile([GRID_AXES, TOKENS], F32, name="grid_rows")
+        nc.sync.dma_start(grid_rows[:], pos[0:GRID_AXES, :])
         offsets = held.tile([P, TOKENS // PER_COLUMN], U16, name="offsets")
         nc.sync.dma_start(offsets[:], offs)
         places = [held.tile([P, TOKENS], F32, name=f"place{a}") for a in range(AXES)]
         words = [held.tile([P, WORDS], F32, name=f"words{b}") for b in range(2 * AXES)]
-        for start in STARTS:
+        for start, b in zip(STARTS, (SEQUENCE, SEQUENCE + AXES)):
             cols = slice(start, start + PIECE)
-            nc.scalar.dma_start(places[SEQUENCE][:, cols], pos[SEQUENCE, cols].partition_broadcast(P))
-        for b in (SEQUENCE, SEQUENCE + AXES):
+            queue = nc.scalar if start == STARTS[0] else nc.sync
+            queue.dma_start(places[SEQUENCE][:, cols], pos[SEQUENCE, cols].partition_broadcast(P))
             nc.sync.dma_start(words[b][:], table[b * P : (b + 1) * P, :])
         for a in range(GRID_AXES):
             nc.sync.dma_start(places[a][:], pos[a, :].partition_broadcast(P))
@@ -101,20 +96,22 @@ def tile_arcembedding_kernel(tc, table, pos, freq, offs, out):
         inverse = held.tile([P, 1], F32, name="inverse")
         nc.vector.reciprocal(inverse[:], places[SEQUENCE][:, TOKENS - 1 : TOKENS])
         pitched = held.tile([P, TOKENS], F32, name="pitched")
+        cosines = [held.tile([P, TOKENS], F32, name=f"cosine{a}") for a in range(AXES)]
+        sines = [held.tile([P, TOKENS], F32, name=f"sine{a}") for a in range(AXES)]
         for start in STARTS:
             cols = slice(start, start + PIECE)
             nc.scalar.activation(pitched[:, cols], places[SEQUENCE][:, cols], COPY, scale=pitch[:])
-
-        last_piece = (ORDER[-1], STARTS[-1])
-        turns = {SEQUENCE: cosine_and_sine(nc, held, pitched, inverse[:], quarter_turn, SEQUENCE)}
+            cosine_and_sine(nc, cosines[SEQUENCE], sines[SEQUENCE], pitched, inverse[:], quarter_turn, cols)
         grid_rates = held.tile([P, GRID_AXES], F32, name="grid_rates")
         nc.scalar.activation(grid_rates[:], spread[:], COPY, scale=pitch[:])
+
+        last_piece = (ORDER[-1], STARTS[-1])
         for a, following in zip(ORDER, ORDER[1:] + (None,)):
             if following is not None:
-                turns[following] = cosine_and_sine(
-                    nc, held, places[following], grid_rates[:, following : following + 1], quarter_turn, following
-                )
-            cosine, sine = turns[a]
+                rate = grid_rates[:, following : following + 1]
+                for start in STARTS:
+                    cols = slice(start, start + PIECE)
+                    cosine_and_sine(nc, cosines[following], sines[following], places[following], rate, quarter_turn, cols)
             low, high = a, a + AXES
             for start in STARTS:
                 cols = slice(start, start + PIECE)
@@ -124,10 +121,10 @@ def tile_arcembedding_kernel(tc, table, pos, freq, offs, out):
                     total = {b: sums.tile([P, PIECE], F32, name="total") for b in (low, high)}
                 products = {}
                 for b, turn, target, signed_unit, first in (
-                    (low, cosine, low, plus, True),
-                    (low, sine, high, plus, True),
-                    (high, cosine, high, plus, False),
-                    (high, sine, low, minus, False),
+                    (low, cosines[a], low, plus, True),
+                    (low, sines[a], high, plus, True),
+                    (high, cosines[a], high, plus, False),
+                    (high, sines[a], low, minus, False),
                 ):
                     product = work.tile([P, PIECE], F32, name=f"product{len(products)}")
                     nc.vector.tensor_tensor(product[:], words[b][:].indirect(picks), turn[:, cols], MULT)

@@ -57,17 +57,6 @@ def tile_arcembedding_kernel(tc, table, pos, freq, offs, out):
             for b in (a, a + AXES):
                 nc.sync.dma_start(words[b][:], table[b * P : (b + 1) * P, :])
 
-        selector = held.tile([GRID_AXES, GRID_AXES * P], F32, name="selector")
-        nc.gpsimd.memset(selector[:], 0.0)
-        nc.gpsimd.affine_select(
-            out=selector[:],
-            in_=selector[:],
-            compare_op=mybir.AluOpType.not_equal,
-            fill=1.0,
-            base=0,
-            pattern=[[-1, GRID_AXES], [0, P]],
-            channel_multiplier=1,
-        )
         plus = held.tile([P, P], F32, name="plus")
         make_identity(nc, plus[:])
         minus = held.tile([P, P], F32, name="minus")
@@ -81,27 +70,33 @@ def tile_arcembedding_kernel(tc, table, pos, freq, offs, out):
             pattern=[[-1, P]],
             channel_multiplier=1,
         )
+        ones = held.tile([GRID_AXES, P], F32, name="ones")
+        nc.vector.memset(ones[:], 1.0)
         quarter_turn = held.tile([P, 1], F32, name="quarter_turn")
         nc.vector.memset(quarter_turn[:], math.pi / 2)
         first_sine = held.tile([P, 1], F32, name="first_sine")
         nc.scalar.activation(first_sine[:], quarter_turn[:], SIN)
 
-        grid_tops = held.tile([GRID_AXES, 1], F32, name="grid_tops")
-        nc.vector.tensor_reduce(grid_tops[:], grid_rows[:], mybir.AxisListType.X, MAX)
-        grid_inverses = held.tile([GRID_AXES, 1], F32, name="grid_inverses")
-        nc.vector.reciprocal(grid_inverses[:], grid_tops[:])
-        spread = once.tile([P, GRID_AXES], F32, name="spread")
-        for a in range(GRID_AXES):
-            nc.tensor.matmul(spread[:, a : a + 1], selector[:, a * P : (a + 1) * P], grid_inverses[:], start=True, stop=True)
         inverse = held.tile([P, 1], F32, name="inverse")
-        nc.vector.reciprocal(inverse[:], places[SEQUENCE][:, TOKENS - 1 : TOKENS])
         pitched = held.tile([P, TOKENS], F32, name="pitched")
         cosines = [held.tile([P, TOKENS], F32, name=f"cosine{a}") for a in range(AXES)]
         sines = [held.tile([P, TOKENS], F32, name=f"sine{a}") for a in range(AXES)]
         for start in STARTS:
             cols = slice(start, start + PIECE)
-            nc.scalar.activation(pitched[:, cols], places[SEQUENCE][:, cols], COPY, scale=pitch[:])
+            if start == STARTS[0]:
+                nc.vector.tensor_scalar(pitched[:, cols], places[SEQUENCE][:, cols], pitch[:], None, MULT)
+                nc.vector.reciprocal(inverse[:], places[SEQUENCE][:, TOKENS - 1 : TOKENS])
+            else:
+                nc.scalar.activation(pitched[:, cols], places[SEQUENCE][:, cols], COPY, scale=pitch[:])
             cosine_and_sine(nc, cosines[SEQUENCE], sines[SEQUENCE], pitched, inverse[:], quarter_turn, cols)
+        grid_tops = held.tile([GRID_AXES, 1], F32, name="grid_tops")
+        nc.vector.tensor_reduce(grid_tops[:], grid_rows[:], mybir.AxisListType.X, MAX)
+        grid_inverses = held.tile([GRID_AXES, 1], F32, name="grid_inverses")
+        nc.vector.reciprocal(grid_inverses[:], grid_tops[:])
+        diagonal = held.tile([GRID_AXES, GRID_AXES], F32, name="diagonal")
+        nc.scalar.activation(diagonal[:], plus[0:GRID_AXES, 0:GRID_AXES], COPY, scale=grid_inverses[:])
+        spread = once.tile([P, GRID_AXES], F32, name="spread")
+        nc.tensor.matmul(spread[:], ones[:], diagonal[:], start=True, stop=True)
         grid_rates = held.tile([P, GRID_AXES], F32, name="grid_rates")
         nc.scalar.activation(grid_rates[:], spread[:], COPY, scale=pitch[:])
 

import math

import concourse.mybir as mybir
from concourse.masks import make_identity

F32 = mybir.dt.float32
U16 = mybir.dt.uint16
MULT = mybir.AluOpType.mult
ADD = mybir.AluOpType.add
SUBTRACT = mybir.AluOpType.subtract
MAX = mybir.AluOpType.max
SIN = mybir.ActivationFunctionType.Sin
COPY = mybir.ActivationFunctionType.Copy

P = 128
WORDS = 256
TOKENS = 512
AXES = 3
GRID_AXES = 2
SEQUENCE = 2
ORDER = (SEQUENCE, 0, 1)
PIECE = 256
STARTS = (TOKENS - PIECE, 0)
PER_COLUMN = 16
PIECES = AXES * len(STARTS)
IN_FLIGHT = 6


def cosine_and_sine(nc, cosine, sine, place, rate, quarter_turn, cols):
    nc.scalar.activation(cosine[:, cols], place[:, cols], SIN, bias=quarter_turn[:], scale=rate)
    nc.scalar.activation(sine[:, cols], place[:, cols], SIN, scale=rate)


def tile_arcembedding_kernel(tc, table, pos, freq, offs, out):
    nc = tc.nc
    with (
        tc.tile_pool(name="held", bufs=1) as held,
        tc.tile_pool(name="work", bufs=PIECES) as work,
        tc.psum_pool(name="sums", bufs=IN_FLIGHT) as sums,
        tc.psum_pool(name="once", bufs=1) as once,
    ):
        pitch = held.tile([P, 1], F32, name="pitch")
        nc.sync.dma_start(pitch[:], freq)
        grid_rows = held.tile([GRID_AXES, TOKENS], F32, name="grid_rows")
        nc.sync.dma_start(grid_rows[:], pos[0:GRID_AXES, :])
        offsets = held.tile([P, TOKENS // PER_COLUMN], U16, name="offsets")
        nc.sync.dma_start(offsets[:], offs)
        places = [held.tile([P, TOKENS], F32, name=f"place{a}") for a in range(AXES)]
        words = [held.tile([P, WORDS], F32, name=f"words{b}") for b in range(2 * AXES)]
        for start, b in zip(STARTS, (SEQUENCE, SEQUENCE + AXES)):
            cols = slice(start, start + PIECE)
            queue = nc.scalar if start == STARTS[0] else nc.sync
            queue.dma_start(places[SEQUENCE][:, cols], pos[SEQUENCE, cols].partition_broadcast(P))
            nc.sync.dma_start(words[b][:], table[b * P : (b + 1) * P, :])
        for a in range(GRID_AXES):
            nc.sync.dma_start(places[a][:], pos[a, :].partition_broadcast(P))
            for b in (a, a + AXES):
                nc.sync.dma_start(words[b][:], table[b * P : (b + 1) * P, :])

        plus = held.tile([P, P], F32, name="plus")
        make_identity(nc, plus[:])
        minus = held.tile([P, P], F32, name="minus")
        nc.gpsimd.memset(minus[:], 0.0)
        nc.gpsimd.affine_select(
            out=minus[:],
            in_=minus[:],
            compare_op=mybir.AluOpType.not_equal,
            fill=-1.0,
            base=0,
            pattern=[[-1, P]],
            channel_multiplier=1,
        )
        ones = held.tile([GRID_AXES, P], F32, name="ones")
        nc.vector.memset(ones[:], 1.0)
        quarter_turn = held.tile([P, 1], F32, name="quarter_turn")
        nc.vector.memset(quarter_turn[:], math.pi / 2)
        first_sine = held.tile([P, 1], F32, name="first_sine")
        nc.scalar.activation(first_sine[:], quarter_turn[:], SIN)

        inverse = held.tile([P, 1], F32, name="inverse")
        pitched = held.tile([P, TOKENS], F32, name="pitched")
        cosines = [held.tile([P, TOKENS], F32, name=f"cosine{a}") for a in range(AXES)]
        sines = [held.tile([P, TOKENS], F32, name=f"sine{a}") for a in range(AXES)]
        for start in STARTS:
            cols = slice(start, start + PIECE)
            if start == STARTS[0]:
                nc.vector.tensor_scalar(pitched[:, cols], places[SEQUENCE][:, cols], pitch[:], None, MULT)
                nc.vector.reciprocal(inverse[:], places[SEQUENCE][:, TOKENS - 1 : TOKENS])
            else:
                nc.scalar.activation(pitched[:, cols], places[SEQUENCE][:, cols], COPY, scale=pitch[:])
            cosine_and_sine(nc, cosines[SEQUENCE], sines[SEQUENCE], pitched, inverse[:], quarter_turn, cols)
        grid_tops = held.tile([GRID_AXES, 1], F32, name="grid_tops")
        nc.vector.tensor_reduce(grid_tops[:], grid_rows[:], mybir.AxisListType.X, MAX)
        grid_inverses = held.tile([GRID_AXES, 1], F32, name="grid_inverses")
        nc.vector.reciprocal(grid_inverses[:], grid_tops[:])
        diagonal = held.tile([GRID_AXES, GRID_AXES], F32, name="diagonal")
        nc.scalar.activation(diagonal[:], plus[0:GRID_AXES, 0:GRID_AXES], COPY, scale=grid_inverses[:])
        spread = once.tile([P, GRID_AXES], F32, name="spread")
        nc.tensor.matmul(spread[:], ones[:], diagonal[:], start=True, stop=True)
        grid_rates = held.tile([P, GRID_AXES], F32, name="grid_rates")
        nc.scalar.activation(grid_rates[:], spread[:], COPY, scale=pitch[:])

        last_piece = (ORDER[-1], STARTS[-1])
        for a, following in zip(ORDER, ORDER[1:] + (None,)):
            if following is not None:
                rate = grid_rates[:, following : following + 1]
                for start in STARTS:
                    cols = slice(start, start + PIECE)
                    cosine_and_sine(nc, cosines[following], sines[following], places[following], rate, quarter_turn, cols)
            low, high = a, a + AXES
            for start in STARTS:
                cols = slice(start, start + PIECE)
                picks = offsets[:, start // PER_COLUMN : (start + PIECE) // PER_COLUMN]
                turned = {b: work.tile([P, PIECE], F32, name=f"turned{b // AXES}") for b in (low, high)}
                if (a, start) != last_piece:
                    total = {b: sums.tile([P, PIECE], F32, name="total") for b in (low, high)}
                products = {}
                for b, turn, target, signed_unit, first in (
                    (low, cosines[a], low, plus, True),
                    (low, sines[a], high, plus, True),
                    (high, cosines[a], high, plus, False),
                    (high, sines[a], low, minus, False),
                ):
                    product = work.tile([P, PIECE], F32, name=f"product{len(products)}")
                    nc.vector.tensor_tensor(product[:], words[b][:].indirect(picks), turn[:, cols], MULT)
                    products[target, first] = product
                    if (a, start) != last_piece:
                        nc.tensor.matmul(total[target][:], signed_unit[:], product[:], start=first, stop=not first)
                for b, signed_op in ((high, ADD), (low, SUBTRACT)):
                    if (a, start) == last_piece:
                        nc.vector.tensor_tensor(turned[b][:], products[b, True][:], products[b, False][:], signed_op)
                    else:
                        nc.scalar.copy(turned[b][:], total[b][:])
                    nc.sync.dma_start(out[b * P : (b + 1) * P, cols], turned[b][:])
